import numpy as np
import ml_dtypes


def mxq(x, axis, fmt="e4m3"):
    dtype, down = {"e4m3": (ml_dtypes.float8_e4m3fn, 7), "e5m2": (ml_dtypes.float8_e5m2, 14)}[fmt]
    v = np.moveaxis(np.asarray(x, np.float32).astype(ml_dtypes.bfloat16).astype(np.float64), axis, -1)
    blocks = v.reshape(v.shape[:-1] + (-1, 32))
    amax = np.abs(blocks).max(-1, keepdims=True)
    byte = np.maximum(np.where(amax > 0, np.frexp(amax)[1] - 1 + 127, 0) - down, 1)
    scale = np.exp2(byte - 127.0)
    codes = (blocks / scale).astype(np.float32).astype(dtype).astype(np.float64)
    return np.moveaxis((codes * scale).reshape(v.shape), -1, axis)


WIDE = False


def mx_kscale(k):
    if not WIDE:
        return np.ones(k)
    levels = np.array([10, -10, 5, -5, 0])
    a = np.random.permutation(np.resize(levels, k // 512 * 4)).reshape(k // 512, 4)
    idx = np.arange(k)
    return np.exp2(a[idx // 512, idx % 128 // 32])


BF16 = ml_dtypes.bfloat16


def bf(x):
    return np.asarray(x, np.float32).astype(BF16)


def f64(x):
    return np.asarray(x).astype(np.float64)


B, H, L, G, P = 128, 1024, 4, 4, 2


def sigmoid(v):
    return 1.0 / (1.0 + np.exp(-v))


def setup_inputs():
    sc = 1.0 / np.sqrt(H)
    th = np.stack([mx_kscale(H) for _ in range(P)], axis=-1)
    si = np.ones((P, H))
    si[0] = mx_kscale(H)
    return {"lstm_input": bf(np.random.standard_normal((B, H)) * 0.3 * si[0]),
            "h0": bf(np.random.standard_normal((B, H, P)) * th),
            "c0": bf(np.random.standard_normal((B, H, P))),
            "W_ih": bf(np.random.standard_normal((P, G * H, H)) * sc / si[:, None, :]),
            "W_hh": bf(np.random.standard_normal((P, G * H, H)) * sc / th.T[:, None, :]),
            "b_ih": bf(np.random.standard_normal((P, G * H)) * 0.3),
            "b_hh": bf(np.random.standard_normal((P, G * H)) * 0.3)}


def reference(lstm_input, h0, c0, W_ih, W_hh, b_ih, b_hh):
    inp = f64(lstm_input)
    h0, c0 = f64(h0), f64(c0)
    W_ih, W_hh, b_ih, b_hh = f64(W_ih), f64(W_hh), f64(b_ih), f64(b_hh)
    hs, cs = [], []
    for j in range(P):
        gates = ((mxq(inp, 1, "e4m3") @ mxq(W_ih[j], 1, "e4m3").T) + b_ih[j]
                 + (mxq(h0[:, :, j], 1, "e4m3") @ mxq(W_hh[j], 1, "e4m3").T) + b_hh[j])
        i, f, g, o = np.split(gates, G, axis=-1)
        i = sigmoid(i)
        f = sigmoid(f)
        g = np.tanh(g)
        o = sigmoid(o)
        c_j = f * c0[:, :, j] + i * g
        h_j = o * np.tanh(c_j)
        inp = h_j
        hs.append(h_j)
        cs.append(c_j)
    return np.stack(hs, axis=-1), np.stack(cs, axis=-1)

@@ -1,0 +1,307 @@
+from contextlib import ExitStack
+
+import concourse.mybir as mybir
+from concourse.masks import make_identity
+
+F32 = mybir.dt.float32
+BF16 = mybir.dt.bfloat16
+U32 = mybir.dt.uint32
+U8 = mybir.dt.uint8
+FP8X4 = mybir.dt.float8_e4m3fn_x4
+ACT = mybir.ActivationFunctionType
+ALU = mybir.AluOpType
+
+P = 128
+H = 1024
+LAYERS = 2
+GATES = 4
+PASSES = H // (4 * P)
+PARITIES = 2
+BLOCK = PARITIES * P
+BLOCKS = H // BLOCK
+ROW_WORDS = H // 2
+BANK = 512
+MATRICES = 2
+
+STEPS = LAYERS * BLOCKS * GATES
+STEP_WORDS = MATRICES * PARITIES * PASSES * P
+
+QUANTISE_LAG = 1
+MULTIPLY_LAG = 2
+UPDATE_LAG = 3
+LOAD_AHEAD = 4
+
+FLOPS = 2 * P * (GATES * H) * (MATRICES * H) * LAYERS
+
+
+def tile_multilayerlstmcell_pb_kernel(
+    tc, lstm_input, h0, c0, W_ih, W_hh, b_ih, b_hh, out_0, out_1
+):
+    nc = tc.nc
+    with ExitStack() as stack:
+        keep = stack.enter_context(tc.tile_pool(name="keep", bufs=1))
+        raw_pool = stack.enter_context(
+            tc.tile_pool(name="raw", bufs=MATRICES * (LOAD_AHEAD + 1))
+        )
+        grouped_pool = stack.enter_context(tc.tile_pool(name="grouped", bufs=3))
+        operand_pool = stack.enter_context(tc.tile_pool(name="operand", bufs=3))
+        gate_pool = stack.enter_context(tc.tile_pool(name="gate", bufs=2))
+        store_pool = stack.enter_context(tc.tile_pool(name="store", bufs=2))
+        bank_pool = stack.enter_context(tc.psum_pool(name="banks", bufs=5))
+        sum_pool = stack.enter_context(tc.psum_pool(name="sums", bufs=3))
+        stack.enter_context(tc.manual_schedule())
+
+        identity = keep.tile([P, P], F32, name="identity")
+        make_identity(nc, identity[:])
+        table_warmer = keep.tile([P, 1], F32, name="table_warmer")
+        nc.scalar.activation(out=table_warmer[:], in_=identity[:, 0:1], func=ACT.Sigmoid)
+
+        def transpose_into_bank(word_blocks):
+            bank = bank_pool.tile([P, BANK], F32, name="bank")
+            for i, block in enumerate(word_blocks):
+                nc.tensor.transpose(bank[:, i * P : (i + 1) * P], block, identity[:])
+            return bank
+
+        def row_blocks(words):
+            return [words[:, w * P : (w + 1) * P] for w in range(ROW_WORDS // P)]
+
+        def regroup(copy, grouped_words, bank):
+            copy(
+                out=grouped_words.rearrange("p (g r u) -> p g r u", g=PASSES, u=2),
+                in_=bank[:].rearrange("p (g u r) -> p g r u", g=PASSES, u=2),
+            )
+
+        def state_blocks(state_words, g):
+            by_parity = state_words.rearrange(
+                "b (w p e) -> b w e p", w=BLOCKS, e=PARITIES
+            )
+            return [by_parity[:, 2 * g + t // 2, t % 2, :] for t in range(4)]
+
+        def moving_operand(name):
+            codes = keep.tile([P, PASSES * P], U32, name=name + "_codes", align_bytes=64)
+            scales = keep.tile([P, PASSES * P], U8, name=name + "_scales", align_bytes=64)
+            return codes, scales
+
+        x_sb = keep.tile([P, H], BF16, name="x_sb")
+        h0_sb = keep.tile([P, H * LAYERS], BF16, name="h0_sb")
+        c0_sb = keep.tile([P, H * LAYERS], BF16, name="c0_sb")
+        bias_rows = keep.tile([P, BLOCK], BF16, name="bias_rows")
+        nc.vector.memset(bias_rows[2 * STEPS : P, :], 0.0)
+        nc.sync.dma_start(out=x_sb[:], in_=lstm_input)
+        nc.sync.dma_start(out=h0_sb[:], in_=h0.rearrange("b h j -> b (h j)"))
+        nc.sync.dma_start(
+            out=bias_rows[0:STEPS, :], in_=b_ih.rearrange("j (s c) -> (j s) c", c=BLOCK)
+        )
+        nc.sync.dma_start(
+            out=bias_rows[STEPS : 2 * STEPS, :],
+            in_=b_hh.rearrange("j (s c) -> (j s) c", c=BLOCK),
+        )
+        nc.sync.dma_start(out=c0_sb[:], in_=c0.rearrange("b h j -> b (h j)"))
+
+        raw_of = {}
+
+        def load(s):
+            j, v, q = s // (BLOCKS * GATES), (s // GATES) % BLOCKS, s % GATES
+            first = q * H + v * BLOCK
+            raw_of[s] = []
+            for weights in (W_hh, W_ih):
+                raw = raw_pool.tile([P, PARITIES * H], BF16, name="raw")
+                nc.sync.dma_start(
+                    out=raw[:],
+                    in_=weights[j, first : first + BLOCK, :].rearrange(
+                        "(r e) k -> r (e k)", e=PARITIES
+                    ),
+                )
+                raw_of[s].append(raw)
+
+        for s in range(LOAD_AHEAD):
+            load(s)
+
+        inputs = [moving_operand("input%d" % j) for j in range(LAYERS)]
+        x_grouped = keep.tile([P, H], BF16, name="x_grouped", align_bytes=64)
+        bank = transpose_into_bank(row_blocks(x_sb[:].bitcast(F32)))
+        regroup(nc.vector.tensor_copy, x_grouped[:].bitcast(F32), bank)
+
+        states = [moving_operand("state%d" % j) for j in range(LAYERS)]
+        h0_grouped = keep.tile([P, LAYERS * H], BF16, name="h0_grouped", align_bytes=64)
+        h0_by_pass = h0_grouped[:].rearrange(
+            "p (j g b t) -> p g j b t", j=LAYERS, g=PASSES, t=4
+        )
+        for g, copy in enumerate((nc.vector.tensor_copy, nc.scalar.copy)):
+            bank = transpose_into_bank(state_blocks(h0_sb[:].bitcast(F32), g))
+            copy(
+                out=h0_by_pass[:, g],
+                in_=bank[:].bitcast(BF16).rearrange("p (t b j) -> p j b t", t=4, j=LAYERS),
+            )
+        nc.vector.quantize_mx(
+            out=inputs[0][0][:].bitcast(FP8X4), scales=inputs[0][1][:], in_=x_grouped[:]
+        )
+        for j in range(LAYERS):
+            nc.vector.quantize_mx(
+                out=states[j][0][:].bitcast(FP8X4),
+                scales=states[j][1][:],
+                in_=h0_grouped[:, j * H : (j + 1) * H],
+            )
+
+        bank = bank_pool.tile([P, BANK], F32, name="bank")
+        nc.tensor.transpose(bank[:, 0:P], bias_rows[:].bitcast(F32), identity[:])
+        bias_pairs = keep.tile([P, PARITIES * P], BF16, name="bias_pairs")
+        nc.vector.tensor_copy(out=bias_pairs[:].bitcast(F32), in_=bank[:, 0:P])
+        bias = keep.tile([P, PARITIES * STEPS], F32, name="bias")
+        nc.vector.tensor_tensor(
+            out=bias[:],
+            in0=bias_pairs[:, 0 : PARITIES * STEPS],
+            in1=bias_pairs[:, PARITIES * STEPS : 2 * PARITIES * STEPS],
+            op=ALU.add,
+        )
+
+        c0_t = keep.tile([P, H * LAYERS], BF16, name="c0_t")
+        for g in range(PASSES):
+            bank = transpose_into_bank(state_blocks(c0_sb[:].bitcast(F32), g))
+            nc.scalar.copy(out=c0_t[:].bitcast(F32)[:, g * BANK : (g + 1) * BANK], in_=bank[:])
+        c0_by_layer = c0_t[:].rearrange("p (n j) -> p j n", j=LAYERS)
+
+        hidden_t = [keep.tile([P, H], F32, name="hidden_t%d" % j) for j in range(LAYERS)]
+        cell_t = [keep.tile([P, H], F32, name="cell_t%d" % j) for j in range(LAYERS)]
+        hidden_grouped = keep.tile([P, H], BF16, name="hidden_grouped", align_bytes=64)
+
+        grouped_of = {}
+        operand_of = {}
+        gates_of = {}
+
+        def transpose(s):
+            grouped = grouped_pool.tile([P, 4 * STEP_WORDS], BF16, name="grouped", align_bytes=64)
+            grouped_words = grouped[:].bitcast(F32)
+            for m in range(MATRICES):
+                words = raw_of[s][m][:].bitcast(F32)
+                for e in range(PARITIES):
+                    n = m * PARITIES + e
+                    bank = transpose_into_bank(
+                        row_blocks(words[:, e * ROW_WORDS : (e + 1) * ROW_WORDS])
+                    )
+                    copy = nc.vector.tensor_copy if n == 0 else nc.scalar.copy
+                    regroup(copy, grouped_words[:, n * BANK : (n + 1) * BANK], bank)
+            grouped_of[s] = grouped
+
+        def quantise(s):
+            codes = operand_pool.tile([P, STEP_WORDS], U32, name="codes", align_bytes=64)
+            scales = operand_pool.tile([P, STEP_WORDS], U8, name="scales", align_bytes=64)
+            nc.vector.quantize_mx(
+                out=codes[:].bitcast(FP8X4), scales=scales[:], in_=grouped_of[s][:]
+            )
+            operand_of[s] = (codes, scales)
+
+        def multiply(s):
+            j, v, q = s // (BLOCKS * GATES), (s // GATES) % BLOCKS, s % GATES
+            codes, scales = operand_of[s]
+            sums = sum_pool.tile([P, PARITIES * P], F32, name="sums")
+            for e in range(PARITIES):
+                for m, (moving_codes, moving_scales) in enumerate((states[j], inputs[j])):
+                    for g in range(PASSES):
+                        first = ((m * PARITIES + e) * PASSES + g) * P
+                        nc.tensor.matmul_mx(
+                            out=sums[:, e * P : (e + 1) * P],
+                            lhsT=codes[:, first : first + P].bitcast(FP8X4),
+                            lhsT_scale=scales[:, first : first + P],
+                            rhs=moving_codes[:, g * P : (g + 1) * P].bitcast(FP8X4),
+                            rhs_scale=moving_scales[:, g * P : (g + 1) * P],
+                            start=(m == 0 and g == 0),
+                            stop=(m == MATRICES - 1 and g == PASSES - 1),
+                        )
+            if q == 0:
+                gates_of[(j, v)] = gate_pool.tile([P, GATES * BLOCK], F32, name="gates")
+            gates = gates_of[(j, v)]
+            if q == 3:
+                tanh_cell = gate_pool.tile([P, BLOCK], F32, name="tanh_cell")
+                nc.scalar.activation(
+                    out=tanh_cell[:],
+                    in_=cell_t[j][:, v * BLOCK : (v + 1) * BLOCK],
+                    func=ACT.Tanh,
+                )
+                gates_of[(j, v, "tanh_cell")] = tanh_cell
+            for e in range(PARITIES):
+                column = ((j * GATES + q) * BLOCKS + v) * PARITIES + e
+                nc.scalar.activation(
+                    out=gates[:, q * BLOCK + e * P : q * BLOCK + (e + 1) * P],
+                    in_=sums[:, e * P : (e + 1) * P],
+                    func=ACT.Tanh if q == 2 else ACT.Sigmoid,
+                    bias=bias[:, column : column + 1],
+                )
+
+        def update(s):
+            j, v, q = s // (BLOCKS * GATES), (s // GATES) % BLOCKS, s % GATES
+            gates = gates_of[(j, v)]
+            block = slice(v * BLOCK, (v + 1) * BLOCK)
+            gate = [gates[:, n * BLOCK : (n + 1) * BLOCK] for n in range(GATES)]
+            if q == 1:
+                kept = gate_pool.tile([P, BLOCK], F32, name="kept")
+                nc.vector.tensor_tensor(
+                    out=kept[:], in0=gate[1], in1=c0_by_layer[:, j, block], op=ALU.mult
+                )
+                gates_of[(j, v, "kept")] = kept
+            if q == 2:
+                fresh = gate_pool.tile([P, BLOCK], F32, name="fresh")
+                nc.vector.tensor_tensor(out=fresh[:], in0=gate[0], in1=gate[2], op=ALU.mult)
+                nc.vector.tensor_tensor(
+                    out=cell_t[j][:, block],
+                    in0=gates_of[(j, v, "kept")][:],
+                    in1=fresh[:],
+                    op=ALU.add,
+                )
+            if q == 3:
+                nc.vector.tensor_tensor(
+                    out=hidden_t[j][:, block],
+                    in0=gate[3],
+                    in1=gates_of[(j, v, "tanh_cell")][:],
+                    op=ALU.mult,
+                )
+            if q == 3 and j == 0 and v % 2 == 1:
+                g = v // 2
+                columns = slice(g * 4 * P, (g + 1) * 4 * P)
+                nc.vector.tensor_copy(
+                    out=hidden_grouped[:, columns].rearrange("p (b t) -> p b t", t=4),
+                    in_=hidden_t[0][:, columns].rearrange("p (t b) -> p b t", t=4),
+                )
+                nc.vector.quantize_mx(
+                    out=inputs[1][0][:, g * P : (g + 1) * P].bitcast(FP8X4),
+                    scales=inputs[1][1][:, g * P : (g + 1) * P],
+                    in_=hidden_grouped[:, columns],
+                )
+
+        def store(s):
+            j, v, q = s // (BLOCKS * GATES), (s // GATES) % BLOCKS, s % GATES
+            if j != LAYERS - 1 or q < 2:
+                return
+            planes, out, copy = (
+                (cell_t, out_1, nc.vector.tensor_copy) if q == 2 else (hidden_t, out_0, nc.scalar.copy)
+            )
+            bank = transpose_into_bank(
+                [
+                    planes[layer][:, (v * PARITIES + e) * P : (v * PARITIES + e + 1) * P]
+                    for e in range(PARITIES)
+                    for layer in range(LAYERS)
+                ]
+            )
+            rows = store_pool.tile([P, BLOCK * LAYERS], F32, name="rows")
+            copy(
+                out=rows[:].rearrange("b (r t) -> b r t", t=4),
+                in_=bank[:].rearrange("b (t r) -> b r t", t=4),
+            )
+            nc.sync.dma_start(
+                out=out[:, v * BLOCK : (v + 1) * BLOCK, :].rearrange("b h j -> b (h j)"),
+                in_=rows[:],
+            )
+
+        for step in range(STEPS + UPDATE_LAG):
+            if step >= UPDATE_LAG:
+                update(step - UPDATE_LAG)
+            if step < STEPS:
+                transpose(step)
+            if step + LOAD_AHEAD < STEPS:
+                load(step + LOAD_AHEAD)
+            if step >= UPDATE_LAG:
+                store(step - UPDATE_LAG)
+            if QUANTISE_LAG <= step < STEPS + QUANTISE_LAG:
+                quantise(step - QUANTISE_LAG)
+            if MULTIPLY_LAG <= step < STEPS + MULTIPLY_LAG:
+                multiply(step - MULTIPLY_LAG)

@@ -28,7 +28,8 @@ STEP_WORDS = MATRICES * PARITIES * PASSES * P
 
 QUANTISE_LAG = 1
 MULTIPLY_LAG = 2
-UPDATE_LAG = 3
+MULTIPLY_EVERY = 2
+UPDATE_LAG = MULTIPLY_LAG + MULTIPLY_EVERY
 LOAD_AHEAD = 4
 
 FLOPS = 2 * P * (GATES * H) * (MATRICES * H) * LAYERS
@@ -44,7 +45,7 @@ def tile_multilayerlstmcell_pb_kernel(
             tc.tile_pool(name="raw", bufs=MATRICES * (LOAD_AHEAD + 1))
         )
         grouped_pool = stack.enter_context(tc.tile_pool(name="grouped", bufs=3))
-        operand_pool = stack.enter_context(tc.tile_pool(name="operand", bufs=3))
+        operand_pool = stack.enter_context(tc.tile_pool(name="operand", bufs=4))
         gate_pool = stack.enter_context(tc.tile_pool(name="gate", bufs=2))
         store_pool = stack.enter_context(tc.tile_pool(name="store", bufs=2))
         bank_pool = stack.enter_context(tc.psum_pool(name="banks", bufs=5))
@@ -87,17 +88,6 @@ def tile_multilayerlstmcell_pb_kernel(
         c0_sb = keep.tile([P, H * LAYERS], BF16, name="c0_sb")
         bias_rows = keep.tile([P, BLOCK], BF16, name="bias_rows")
         nc.vector.memset(bias_rows[2 * STEPS : P, :], 0.0)
-        nc.sync.dma_start(out=x_sb[:], in_=lstm_input)
-        nc.sync.dma_start(out=h0_sb[:], in_=h0.rearrange("b h j -> b (h j)"))
-        nc.sync.dma_start(
-            out=bias_rows[0:STEPS, :], in_=b_ih.rearrange("j (s c) -> (j s) c", c=BLOCK)
-        )
-        nc.sync.dma_start(
-            out=bias_rows[STEPS : 2 * STEPS, :],
-            in_=b_hh.rearrange("j (s c) -> (j s) c", c=BLOCK),
-        )
-        nc.sync.dma_start(out=c0_sb[:], in_=c0.rearrange("b h j -> b (h j)"))
-
         raw_of = {}
 
         def load(s):
@@ -114,7 +104,18 @@ def tile_multilayerlstmcell_pb_kernel(
                 )
                 raw_of[s].append(raw)
 
-        for s in range(LOAD_AHEAD):
+        nc.sync.dma_start(out=x_sb[:], in_=lstm_input)
+        nc.sync.dma_start(out=h0_sb[:], in_=h0.rearrange("b h j -> b (h j)"))
+        load(0)
+        nc.sync.dma_start(
+            out=bias_rows[0:STEPS, :], in_=b_ih.rearrange("j (s c) -> (j s) c", c=BLOCK)
+        )
+        nc.sync.dma_start(
+            out=bias_rows[STEPS : 2 * STEPS, :],
+            in_=b_hh.rearrange("j (s c) -> (j s) c", c=BLOCK),
+        )
+        nc.sync.dma_start(out=c0_sb[:], in_=c0.rearrange("b h j -> b (h j)"))
+        for s in range(1, LOAD_AHEAD):
             load(s)
 
         inputs = [moving_operand("input%d" % j) for j in range(LAYERS)]
@@ -143,23 +144,26 @@ def tile_multilayerlstmcell_pb_kernel(
                 in_=h0_grouped[:, j * H : (j + 1) * H],
             )
 
-        bank = bank_pool.tile([P, BANK], F32, name="bank")
-        nc.tensor.transpose(bank[:, 0:P], bias_rows[:].bitcast(F32), identity[:])
         bias_pairs = keep.tile([P, PARITIES * P], BF16, name="bias_pairs")
-        nc.vector.tensor_copy(out=bias_pairs[:].bitcast(F32), in_=bank[:, 0:P])
         bias = keep.tile([P, PARITIES * STEPS], F32, name="bias")
-        nc.vector.tensor_tensor(
-            out=bias[:],
-            in0=bias_pairs[:, 0 : PARITIES * STEPS],
-            in1=bias_pairs[:, PARITIES * STEPS : 2 * PARITIES * STEPS],
-            op=ALU.add,
-        )
-
         c0_t = keep.tile([P, H * LAYERS], BF16, name="c0_t")
-        for g in range(PASSES):
-            bank = transpose_into_bank(state_blocks(c0_sb[:].bitcast(F32), g))
-            nc.scalar.copy(out=c0_t[:].bitcast(F32)[:, g * BANK : (g + 1) * BANK], in_=bank[:])
         c0_by_layer = c0_t[:].rearrange("p (n j) -> p j n", j=LAYERS)
+
+        def transpose_bias_and_cell():
+            pairs_bank = bank_pool.tile([P, BANK], F32, name="bank")
+            nc.tensor.transpose(pairs_bank[:, 0:P], bias_rows[:].bitcast(F32), identity[:])
+            nc.vector.tensor_copy(out=bias_pairs[:].bitcast(F32), in_=pairs_bank[:, 0:P])
+            nc.vector.tensor_tensor(
+                out=bias[:],
+                in0=bias_pairs[:, 0 : PARITIES * STEPS],
+                in1=bias_pairs[:, PARITIES * STEPS : 2 * PARITIES * STEPS],
+                op=ALU.add,
+            )
+            for g in range(PASSES):
+                cell_bank = transpose_into_bank(state_blocks(c0_sb[:].bitcast(F32), g))
+                nc.scalar.copy(
+                    out=c0_t[:].bitcast(F32)[:, g * BANK : (g + 1) * BANK], in_=cell_bank[:]
+                )
 
         hidden_t = [keep.tile([P, H], F32, name="hidden_t%d" % j) for j in range(LAYERS)]
         cell_t = [keep.tile([P, H], F32, name="cell_t%d" % j) for j in range(LAYERS)]
@@ -211,14 +215,6 @@ def tile_multilayerlstmcell_pb_kernel(
             if q == 0:
                 gates_of[(j, v)] = gate_pool.tile([P, GATES * BLOCK], F32, name="gates")
             gates = gates_of[(j, v)]
-            if q == 3:
-                tanh_cell = gate_pool.tile([P, BLOCK], F32, name="tanh_cell")
-                nc.scalar.activation(
-                    out=tanh_cell[:],
-                    in_=cell_t[j][:, v * BLOCK : (v + 1) * BLOCK],
-                    func=ACT.Tanh,
-                )
-                gates_of[(j, v, "tanh_cell")] = tanh_cell
             for e in range(PARITIES):
                 column = ((j * GATES + q) * BLOCKS + v) * PARITIES + e
                 nc.scalar.activation(
@@ -268,6 +264,16 @@ def tile_multilayerlstmcell_pb_kernel(
                     in_=hidden_grouped[:, columns],
                 )
 
+        def squash(s):
+            j, v, q = s // (BLOCKS * GATES), (s // GATES) % BLOCKS, s % GATES
+            if q != 2:
+                return
+            tanh_cell = gate_pool.tile([P, BLOCK], F32, name="tanh_cell")
+            nc.scalar.activation(
+                out=tanh_cell[:], in_=cell_t[j][:, v * BLOCK : (v + 1) * BLOCK], func=ACT.Tanh
+            )
+            gates_of[(j, v, "tanh_cell")] = tanh_cell
+
         def store(s):
             j, v, q = s // (BLOCKS * GATES), (s // GATES) % BLOCKS, s % GATES
             if j != LAYERS - 1 or q < 2:
@@ -292,16 +298,22 @@ def tile_multilayerlstmcell_pb_kernel(
                 in_=rows[:],
             )
 
+        multiplied = 0
         for step in range(STEPS + UPDATE_LAG):
             if step >= UPDATE_LAG:
                 update(step - UPDATE_LAG)
             if step < STEPS:
                 transpose(step)
+            if step == 0:
+                transpose_bias_and_cell()
             if step + LOAD_AHEAD < STEPS:
                 load(step + LOAD_AHEAD)
             if step >= UPDATE_LAG:
                 store(step - UPDATE_LAG)
+                squash(step - UPDATE_LAG)
             if QUANTISE_LAG <= step < STEPS + QUANTISE_LAG:
                 quantise(step - QUANTISE_LAG)
-            if MULTIPLY_LAG <= step < STEPS + MULTIPLY_LAG:
-                multiply(step - MULTIPLY_LAG)
+            if (step + 1) % MULTIPLY_EVERY == 0 or step >= STEPS:
+                while multiplied < min(step - MULTIPLY_LAG + 1, STEPS):
+                    multiply(multiplied)
+                    multiplied += 1

@@ -24,12 +24,12 @@ BANK = 512
 MATRICES = 2
 
 STEPS = LAYERS * BLOCKS * GATES
-STEP_WORDS = MATRICES * PARITIES * PASSES * P
+MATRIX_WORDS = PARITIES * PASSES * P
+STEP_WORDS = MATRICES * MATRIX_WORDS
 
 QUANTISE_LAG = 1
 MULTIPLY_LAG = 2
-MULTIPLY_EVERY = 2
-UPDATE_LAG = MULTIPLY_LAG + MULTIPLY_EVERY
+UPDATE_LAG = 3
 LOAD_AHEAD = 4
 
 FLOPS = 2 * P * (GATES * H) * (MATRICES * H) * LAYERS
@@ -47,7 +47,7 @@ def tile_multilayerlstmcell_pb_kernel(
         grouped_pool = stack.enter_context(tc.tile_pool(name="grouped", bufs=3))
         operand_pool = stack.enter_context(tc.tile_pool(name="operand", bufs=4))
         gate_pool = stack.enter_context(tc.tile_pool(name="gate", bufs=2))
-        store_pool = stack.enter_context(tc.tile_pool(name="store", bufs=2))
+        store_pool = stack.enter_context(tc.tile_pool(name="store", bufs=2 * BLOCKS))
         bank_pool = stack.enter_context(tc.psum_pool(name="banks", bufs=5))
         sum_pool = stack.enter_context(tc.psum_pool(name="sums", bufs=3))
         stack.enter_context(tc.manual_schedule())
@@ -183,16 +183,20 @@ def tile_multilayerlstmcell_pb_kernel(
                     bank = transpose_into_bank(
                         row_blocks(words[:, e * ROW_WORDS : (e + 1) * ROW_WORDS])
                     )
-                    copy = nc.vector.tensor_copy if n == 0 else nc.scalar.copy
+                    copy = nc.vector.tensor_copy if n == MATRICES * PARITIES - 1 else nc.scalar.copy
                     regroup(copy, grouped_words[:, n * BANK : (n + 1) * BANK], bank)
             grouped_of[s] = grouped
 
         def quantise(s):
             codes = operand_pool.tile([P, STEP_WORDS], U32, name="codes", align_bytes=64)
             scales = operand_pool.tile([P, STEP_WORDS], U8, name="scales", align_bytes=64)
-            nc.vector.quantize_mx(
-                out=codes[:].bitcast(FP8X4), scales=scales[:], in_=grouped_of[s][:]
-            )
+            for m in range(MATRICES):
+                first, last = m * MATRIX_WORDS, (m + 1) * MATRIX_WORDS
+                nc.vector.quantize_mx(
+                    out=codes[:, first:last].bitcast(FP8X4),
+                    scales=scales[:, first:last],
+                    in_=grouped_of[s][:, 4 * first : 4 * last],
+                )
             operand_of[s] = (codes, scales)
 
         def multiply(s):
@@ -274,46 +278,45 @@ def tile_multilayerlstmcell_pb_kernel(
             )
             gates_of[(j, v, "tanh_cell")] = tanh_cell
 
-        def store(s):
-            j, v, q = s // (BLOCKS * GATES), (s // GATES) % BLOCKS, s % GATES
-            if j != LAYERS - 1 or q < 2:
-                return
-            planes, out, copy = (
-                (cell_t, out_1, nc.vector.tensor_copy) if q == 2 else (hidden_t, out_0, nc.scalar.copy)
-            )
-            bank = transpose_into_bank(
-                [
-                    planes[layer][:, (v * PARITIES + e) * P : (v * PARITIES + e + 1) * P]
-                    for e in range(PARITIES)
-                    for layer in range(LAYERS)
-                ]
-            )
-            rows = store_pool.tile([P, BLOCK * LAYERS], F32, name="rows")
-            copy(
-                out=rows[:].rearrange("b (r t) -> b r t", t=4),
-                in_=bank[:].rearrange("b (t r) -> b r t", t=4),
-            )
-            nc.sync.dma_start(
-                out=out[:, v * BLOCK : (v + 1) * BLOCK, :].rearrange("b h j -> b (h j)"),
-                in_=rows[:],
-            )
+        finished = []
 
-        multiplied = 0
+        def transpose_back(s):
+            j, v, q = s // (BLOCKS * GATES), (s // GATES) % BLOCKS, s % GATES
+            if j != LAYERS - 1 or q != GATES - 1:
+                return
+            for planes, out, copy in (
+                (cell_t, out_1, nc.vector.tensor_copy),
+                (hidden_t, out_0, nc.scalar.copy),
+            ):
+                bank = transpose_into_bank(
+                    [
+                        planes[layer][:, (v * PARITIES + e) * P : (v * PARITIES + e + 1) * P]
+                        for e in range(PARITIES)
+                        for layer in range(LAYERS)
+                    ]
+                )
+                rows = store_pool.tile([P, BLOCK * LAYERS], F32, name="rows")
+                copy(
+                    out=rows[:].rearrange("b (r t) -> b r t", t=4),
+                    in_=bank[:].rearrange("b (t r) -> b r t", t=4),
+                )
+                finished.append((out[:, v * BLOCK : (v + 1) * BLOCK, :], rows))
+
         for step in range(STEPS + UPDATE_LAG):
             if step >= UPDATE_LAG:
                 update(step - UPDATE_LAG)
+            if QUANTISE_LAG <= step < STEPS + QUANTISE_LAG:
+                quantise(step - QUANTISE_LAG)
             if step < STEPS:
                 transpose(step)
             if step == 0:
                 transpose_bias_and_cell()
             if step + LOAD_AHEAD < STEPS:
                 load(step + LOAD_AHEAD)
+            if MULTIPLY_LAG <= step < STEPS + MULTIPLY_LAG:
+                multiply(step - MULTIPLY_LAG)
             if step >= UPDATE_LAG:
-                store(step - UPDATE_LAG)
                 squash(step - UPDATE_LAG)
-            if QUANTISE_LAG <= step < STEPS + QUANTISE_LAG:
-                quantise(step - QUANTISE_LAG)
-            if (step + 1) % MULTIPLY_EVERY == 0 or step >= STEPS:
-                while multiplied < min(step - MULTIPLY_LAG + 1, STEPS):
-                    multiply(multiplied)
-                    multiplied += 1
+                transpose_back(step - UPDATE_LAG)
+        for out_rows, rows in finished:
+            nc.sync.dma_start(out=out_rows.rearrange("b h j -> b (h j)"), in_=rows[:])

@@ -27,9 +27,6 @@ STEPS = LAYERS * BLOCKS * GATES
 MATRIX_WORDS = PARITIES * PASSES * P
 STEP_WORDS = MATRICES * MATRIX_WORDS
 
-QUANTISE_LAG = 1
-MULTIPLY_LAG = 2
-UPDATE_LAG = 3
 LOAD_AHEAD = 4
 
 FLOPS = 2 * P * (GATES * H) * (MATRICES * H) * LAYERS
@@ -96,17 +93,20 @@ def tile_multilayerlstmcell_pb_kernel(
             raw_of[s] = []
             for weights in (W_hh, W_ih):
                 raw = raw_pool.tile([P, PARITIES * H], BF16, name="raw")
-                nc.sync.dma_start(
-                    out=raw[:],
-                    in_=weights[j, first : first + BLOCK, :].rearrange(
-                        "(r e) k -> r (e k)", e=PARITIES
-                    ),
+                rows = weights[j, first : first + BLOCK, :].rearrange(
+                    "(r e) k -> r (e k)", e=PARITIES
                 )
+                pieces = PARITIES if s == 0 and not raw_of[s] else 1
+                width = PARITIES * H // pieces
+                for n in range(pieces):
+                    columns = slice(n * width, (n + 1) * width)
+                    nc.sync.dma_start(out=raw[:, columns], in_=rows[:, columns])
                 raw_of[s].append(raw)
 
+        load(0)
         nc.sync.dma_start(out=x_sb[:], in_=lstm_input)
         nc.sync.dma_start(out=h0_sb[:], in_=h0.rearrange("b h j -> b (h j)"))
-        load(0)
+        load(1)
         nc.sync.dma_start(
             out=bias_rows[0:STEPS, :], in_=b_ih.rearrange("j (s c) -> (j s) c", c=BLOCK)
         )
@@ -115,34 +115,35 @@ def tile_multilayerlstmcell_pb_kernel(
             in_=b_hh.rearrange("j (s c) -> (j s) c", c=BLOCK),
         )
         nc.sync.dma_start(out=c0_sb[:], in_=c0.rearrange("b h j -> b (h j)"))
-        for s in range(1, LOAD_AHEAD):
+        for s in range(2, LOAD_AHEAD):
             load(s)
 
         inputs = [moving_operand("input%d" % j) for j in range(LAYERS)]
-        x_grouped = keep.tile([P, H], BF16, name="x_grouped", align_bytes=64)
-        bank = transpose_into_bank(row_blocks(x_sb[:].bitcast(F32)))
-        regroup(nc.vector.tensor_copy, x_grouped[:].bitcast(F32), bank)
-
         states = [moving_operand("state%d" % j) for j in range(LAYERS)]
+        x_grouped = keep.tile([P, H], BF16, name="x_grouped", align_bytes=64)
         h0_grouped = keep.tile([P, LAYERS * H], BF16, name="h0_grouped", align_bytes=64)
-        h0_by_pass = h0_grouped[:].rearrange(
-            "p (j g b t) -> p g j b t", j=LAYERS, g=PASSES, t=4
-        )
-        for g, copy in enumerate((nc.vector.tensor_copy, nc.scalar.copy)):
-            bank = transpose_into_bank(state_blocks(h0_sb[:].bitcast(F32), g))
-            copy(
-                out=h0_by_pass[:, g],
-                in_=bank[:].bitcast(BF16).rearrange("p (t b j) -> p j b t", t=4, j=LAYERS),
+
+        def make_moving_operands():
+            bank = transpose_into_bank(row_blocks(x_sb[:].bitcast(F32)))
+            regroup(nc.vector.tensor_copy, x_grouped[:].bitcast(F32), bank)
+            h0_by_pass = h0_grouped[:].rearrange(
+                "p (j g b t) -> p g j b t", j=LAYERS, g=PASSES, t=4
             )
-        nc.vector.quantize_mx(
-            out=inputs[0][0][:].bitcast(FP8X4), scales=inputs[0][1][:], in_=x_grouped[:]
-        )
-        for j in range(LAYERS):
+            for g, copy in enumerate((nc.vector.tensor_copy, nc.scalar.copy)):
+                bank = transpose_into_bank(state_blocks(h0_sb[:].bitcast(F32), g))
+                copy(
+                    out=h0_by_pass[:, g],
+                    in_=bank[:].bitcast(BF16).rearrange("p (t b j) -> p j b t", t=4, j=LAYERS),
+                )
             nc.vector.quantize_mx(
-                out=states[j][0][:].bitcast(FP8X4),
-                scales=states[j][1][:],
-                in_=h0_grouped[:, j * H : (j + 1) * H],
+                out=inputs[0][0][:].bitcast(FP8X4), scales=inputs[0][1][:], in_=x_grouped[:]
             )
+            for j in range(LAYERS):
+                nc.vector.quantize_mx(
+                    out=states[j][0][:].bitcast(FP8X4),
+                    scales=states[j][1][:],
+                    in_=h0_grouped[:, j * H : (j + 1) * H],
+                )
 
         bias_pairs = keep.tile([P, PARITIES * P], BF16, name="bias_pairs")
         bias = keep.tile([P, PARITIES * STEPS], F32, name="bias")
@@ -172,43 +173,52 @@ def tile_multilayerlstmcell_pb_kernel(
         grouped_of = {}
         operand_of = {}
         gates_of = {}
+        sums_of = {}
 
-        def transpose(s):
-            grouped = grouped_pool.tile([P, 4 * STEP_WORDS], BF16, name="grouped", align_bytes=64)
-            grouped_words = grouped[:].bitcast(F32)
-            for m in range(MATRICES):
-                words = raw_of[s][m][:].bitcast(F32)
-                for e in range(PARITIES):
-                    n = m * PARITIES + e
-                    bank = transpose_into_bank(
-                        row_blocks(words[:, e * ROW_WORDS : (e + 1) * ROW_WORDS])
-                    )
-                    copy = nc.vector.tensor_copy if n == MATRICES * PARITIES - 1 else nc.scalar.copy
-                    regroup(copy, grouped_words[:, n * BANK : (n + 1) * BANK], bank)
-            grouped_of[s] = grouped
+        def place(s):
+            return s // (BLOCKS * GATES), (s // GATES) % BLOCKS, s % GATES
 
-        def quantise(s):
-            codes = operand_pool.tile([P, STEP_WORDS], U32, name="codes", align_bytes=64)
-            scales = operand_pool.tile([P, STEP_WORDS], U8, name="scales", align_bytes=64)
-            for m in range(MATRICES):
-                first, last = m * MATRIX_WORDS, (m + 1) * MATRIX_WORDS
-                nc.vector.quantize_mx(
-                    out=codes[:, first:last].bitcast(FP8X4),
-                    scales=scales[:, first:last],
-                    in_=grouped_of[s][:, 4 * first : 4 * last],
+        def transpose(s, m, shared=False):
+            if s not in grouped_of:
+                grouped_of[s] = grouped_pool.tile(
+                    [P, 4 * STEP_WORDS], BF16, name="grouped", align_bytes=64
                 )
-            operand_of[s] = (codes, scales)
+            grouped_words = grouped_of[s][:].bitcast(F32)
+            words = raw_of[s][m][:].bitcast(F32)
+            for e in range(PARITIES):
+                n = m * PARITIES + e
+                bank = transpose_into_bank(
+                    row_blocks(words[:, e * ROW_WORDS : (e + 1) * ROW_WORDS])
+                )
+                on_vector = n % 2 == 1 if shared else n == MATRICES * PARITIES - 1
+                copy = nc.vector.tensor_copy if on_vector else nc.scalar.copy
+                regroup(copy, grouped_words[:, n * BANK : (n + 1) * BANK], bank)
+
+        def quantise(s, m):
+            if s not in operand_of:
+                codes = operand_pool.tile([P, STEP_WORDS], U32, name="codes", align_bytes=64)
+                scales = operand_pool.tile([P, STEP_WORDS], U8, name="scales", align_bytes=64)
+                operand_of[s] = (codes, scales)
+            codes, scales = operand_of[s]
+            first, last = m * MATRIX_WORDS, (m + 1) * MATRIX_WORDS
+            nc.vector.quantize_mx(
+                out=codes[:, first:last].bitcast(FP8X4),
+                scales=scales[:, first:last],
+                in_=grouped_of[s][:, 4 * first : 4 * last],
+            )
 
         def multiply(s):
-            j, v, q = s // (BLOCKS * GATES), (s // GATES) % BLOCKS, s % GATES
+            j, v, q = place(s)
             codes, scales = operand_of[s]
             sums = sum_pool.tile([P, PARITIES * P], F32, name="sums")
+            sums_of[s] = sums
             for e in range(PARITIES):
+                column = e * P
                 for m, (moving_codes, moving_scales) in enumerate((states[j], inputs[j])):
                     for g in range(PASSES):
                         first = ((m * PARITIES + e) * PASSES + g) * P
                         nc.tensor.matmul_mx(
-                            out=sums[:, e * P : (e + 1) * P],
+                            out=sums[:, column : column + P],
                             lhsT=codes[:, first : first + P].bitcast(FP8X4),
                             lhsT_scale=scales[:, first : first + P],
                             rhs=moving_codes[:, g * P : (g + 1) * P].bitcast(FP8X4),
@@ -216,107 +226,175 @@ def tile_multilayerlstmcell_pb_kernel(
                             start=(m == 0 and g == 0),
                             stop=(m == MATRICES - 1 and g == PASSES - 1),
                         )
+
+        def activate(s):
+            j, v, q = place(s)
             if q == 0:
                 gates_of[(j, v)] = gate_pool.tile([P, GATES * BLOCK], F32, name="gates")
             gates = gates_of[(j, v)]
             for e in range(PARITIES):
-                column = ((j * GATES + q) * BLOCKS + v) * PARITIES + e
+                column = e * P
+                step_bias = ((j * GATES + q) * BLOCKS + v) * PARITIES + e
                 nc.scalar.activation(
                     out=gates[:, q * BLOCK + e * P : q * BLOCK + (e + 1) * P],
-                    in_=sums[:, e * P : (e + 1) * P],
+                    in_=sums_of[s][:, column : column + P],
                     func=ACT.Tanh if q == 2 else ACT.Sigmoid,
-                    bias=bias[:, column : column + 1],
+                    bias=bias[:, step_bias : step_bias + 1],
                 )
 
-        def update(s):
-            j, v, q = s // (BLOCKS * GATES), (s // GATES) % BLOCKS, s % GATES
-            gates = gates_of[(j, v)]
-            block = slice(v * BLOCK, (v + 1) * BLOCK)
-            gate = [gates[:, n * BLOCK : (n + 1) * BLOCK] for n in range(GATES)]
-            if q == 1:
-                kept = gate_pool.tile([P, BLOCK], F32, name="kept")
-                nc.vector.tensor_tensor(
-                    out=kept[:], in0=gate[1], in1=c0_by_layer[:, j, block], op=ALU.mult
-                )
-                gates_of[(j, v, "kept")] = kept
-            if q == 2:
-                fresh = gate_pool.tile([P, BLOCK], F32, name="fresh")
-                nc.vector.tensor_tensor(out=fresh[:], in0=gate[0], in1=gate[2], op=ALU.mult)
-                nc.vector.tensor_tensor(
-                    out=cell_t[j][:, block],
-                    in0=gates_of[(j, v, "kept")][:],
-                    in1=fresh[:],
-                    op=ALU.add,
-                )
-            if q == 3:
-                nc.vector.tensor_tensor(
-                    out=hidden_t[j][:, block],
-                    in0=gate[3],
-                    in1=gates_of[(j, v, "tanh_cell")][:],
-                    op=ALU.mult,
-                )
-            if q == 3 and j == 0 and v % 2 == 1:
-                g = v // 2
-                columns = slice(g * 4 * P, (g + 1) * 4 * P)
-                nc.vector.tensor_copy(
-                    out=hidden_grouped[:, columns].rearrange("p (b t) -> p b t", t=4),
-                    in_=hidden_t[0][:, columns].rearrange("p (t b) -> p b t", t=4),
-                )
-                nc.vector.quantize_mx(
-                    out=inputs[1][0][:, g * P : (g + 1) * P].bitcast(FP8X4),
-                    scales=inputs[1][1][:, g * P : (g + 1) * P],
-                    in_=hidden_grouped[:, columns],
-                )
+        def gate(j, v, q):
+            return gates_of[(j, v)][:, q * BLOCK : (q + 1) * BLOCK]
 
-        def squash(s):
-            j, v, q = s // (BLOCKS * GATES), (s // GATES) % BLOCKS, s % GATES
-            if q != 2:
-                return
-            tanh_cell = gate_pool.tile([P, BLOCK], F32, name="tanh_cell")
-            nc.scalar.activation(
-                out=tanh_cell[:], in_=cell_t[j][:, v * BLOCK : (v + 1) * BLOCK], func=ACT.Tanh
+        def block_of(planes, j, v):
+            return planes[j][:, v * BLOCK : (v + 1) * BLOCK]
+
+        def keep_cell(j, v):
+            kept = gate_pool.tile([P, BLOCK], F32, name="kept")
+            nc.vector.tensor_tensor(
+                out=kept[:],
+                in0=gate(j, v, 1),
+                in1=c0_by_layer[:, j, v * BLOCK : (v + 1) * BLOCK],
+                op=ALU.mult,
             )
+            gates_of[(j, v, "kept")] = kept
+
+        def make_fresh(j, v):
+            fresh = gate_pool.tile([P, BLOCK], F32, name="fresh")
+            nc.vector.tensor_tensor(
+                out=fresh[:], in0=gate(j, v, 0), in1=gate(j, v, 2), op=ALU.mult
+            )
+            gates_of[(j, v, "fresh")] = fresh
+
+        def add_cell(j, v):
+            nc.vector.tensor_tensor(
+                out=block_of(cell_t, j, v),
+                in0=gates_of[(j, v, "kept")][:],
+                in1=gates_of[(j, v, "fresh")][:],
+                op=ALU.add,
+            )
+
+        def squash(j, v):
+            tanh_cell = gate_pool.tile([P, BLOCK], F32, name="tanh_cell")
+            nc.scalar.activation(out=tanh_cell[:], in_=block_of(cell_t, j, v), func=ACT.Tanh)
             gates_of[(j, v, "tanh_cell")] = tanh_cell
+
+        def make_hidden(j, v):
+            nc.vector.tensor_tensor(
+                out=block_of(hidden_t, j, v),
+                in0=gate(j, v, 3),
+                in1=gates_of[(j, v, "tanh_cell")][:],
+                op=ALU.mult,
+            )
+
+        def group_hidden(g):
+            columns = slice(g * 4 * P, (g + 1) * 4 * P)
+            nc.vector.tensor_copy(
+                out=hidden_grouped[:, columns].rearrange("p (b t) -> p b t", t=4),
+                in_=hidden_t[0][:, columns].rearrange("p (t b) -> p b t", t=4),
+            )
+
+        def quantise_hidden(g):
+            nc.vector.quantize_mx(
+                out=inputs[1][0][:, g * P : (g + 1) * P].bitcast(FP8X4),
+                scales=inputs[1][1][:, g * P : (g + 1) * P],
+                in_=hidden_grouped[:, g * 4 * P : (g + 1) * 4 * P],
+            )
 
         finished = []
 
-        def transpose_back(s):
-            j, v, q = s // (BLOCKS * GATES), (s // GATES) % BLOCKS, s % GATES
-            if j != LAYERS - 1 or q != GATES - 1:
-                return
-            for planes, out, copy in (
-                (cell_t, out_1, nc.vector.tensor_copy),
-                (hidden_t, out_0, nc.scalar.copy),
-            ):
-                bank = transpose_into_bank(
-                    [
-                        planes[layer][:, (v * PARITIES + e) * P : (v * PARITIES + e + 1) * P]
-                        for e in range(PARITIES)
-                        for layer in range(LAYERS)
-                    ]
-                )
-                rows = store_pool.tile([P, BLOCK * LAYERS], F32, name="rows")
-                copy(
-                    out=rows[:].rearrange("b (r t) -> b r t", t=4),
-                    in_=bank[:].rearrange("b (t r) -> b r t", t=4),
-                )
-                finished.append((out[:, v * BLOCK : (v + 1) * BLOCK, :], rows))
+        def transpose_back(v, planes, out, copy):
+            bank = transpose_into_bank(
+                [
+                    planes[layer][:, (v * PARITIES + e) * P : (v * PARITIES + e + 1) * P]
+                    for e in range(PARITIES)
+                    for layer in range(LAYERS)
+                ]
+            )
+            rows = store_pool.tile([P, BLOCK * LAYERS], F32, name="rows")
+            copy(
+                out=rows[:].rearrange("b (r t) -> b r t", t=4),
+                in_=bank[:].rearrange("b (t r) -> b r t", t=4),
+            )
+            finished.append((out[:, v * BLOCK : (v + 1) * BLOCK, :], rows))
 
-        for step in range(STEPS + UPDATE_LAG):
-            if step >= UPDATE_LAG:
-                update(step - UPDATE_LAG)
-            if QUANTISE_LAG <= step < STEPS + QUANTISE_LAG:
-                quantise(step - QUANTISE_LAG)
-            if step < STEPS:
-                transpose(step)
-            if step == 0:
+        def cell_back(v, copy=nc.vector.tensor_copy):
+            transpose_back(v, cell_t, out_1, copy)
+
+        def hidden_back(v):
+            transpose_back(v, hidden_t, out_0, nc.scalar.copy)
+
+        UPPER = BLOCKS * GATES
+        LAST = STEPS - 1
+
+        def update_first(s):
+            j, v, q = place(s)
+            if s == UPPER or (j == 0 and q == 0 and v == 2):
+                quantise_hidden(0 if s < UPPER else 1)
+            if q == 1:
+                keep_cell(j, v)
+            if q == 2:
+                make_fresh(j, v)
+            if q == 3:
+                make_hidden(j, v)
+
+        def update_last(s):
+            j, v, q = place(s)
+            if q == 2:
+                add_cell(j, v)
+            if q == 3 and j == 0 and v % 2 == 1:
+                group_hidden(v // 2)
+
+        for s in range(LAST):
+            if s >= 1:
+                for m in range(MATRICES):
+                    quantise(s - 1, m)
+            if s >= 3:
+                update_first(s - 3)
+            for m in range(MATRICES):
+                transpose(s, m, shared=s == 0)
+            if s == 0:
+                make_moving_operands()
+            if s == 1:
                 transpose_bias_and_cell()
-            if step + LOAD_AHEAD < STEPS:
-                load(step + LOAD_AHEAD)
-            if MULTIPLY_LAG <= step < STEPS + MULTIPLY_LAG:
-                multiply(step - MULTIPLY_LAG)
-            if step >= UPDATE_LAG:
-                squash(step - UPDATE_LAG)
-                transpose_back(step - UPDATE_LAG)
+            if s + LOAD_AHEAD < STEPS:
+                load(s + LOAD_AHEAD)
+            if s >= 3:
+                update_last(s - 3)
+            ripe = [] if s - 2 == UPPER else [s - 2] if s - 2 != UPPER + 1 else [s - 3, s - 2]
+            for r in ripe:
+                if r >= 0:
+                    multiply(r)
+            for r in ripe:
+                if r >= 0:
+                    activate(r)
+            if s >= 3:
+                j, v, q = place(s - 3)
+                if q == 2:
+                    squash(j, v)
+                if q == 3 and j == 1 and v < BLOCKS - 2:
+                    hidden_back(v)
+                    cell_back(v)
+        top = (LAYERS - 1, BLOCKS - 1)
+        for m in range(MATRICES):
+            quantise(LAST - 1, m)
+        transpose(LAST, 0, shared=True)
+        multiply(LAST - 2)
+        activate(LAST - 2)
+        transpose(LAST, 1, shared=True)
+        multiply(LAST - 1)
+        activate(LAST - 1)
+        hidden_back(BLOCKS - 2)
+        cell_back(BLOCKS - 2, nc.scalar.copy)
+        keep_cell(*top)
+        quantise(LAST, 0)
+        make_fresh(*top)
+        quantise(LAST, 1)
+        add_cell(*top)
+        multiply(LAST)
+        squash(*top)
+        activate(LAST)
+        make_hidden(*top)
+        cell_back(BLOCKS - 1)
+        hidden_back(BLOCKS - 1)
         for out_rows, rows in finished:
             nc.sync.dma_start(out=out_rows.rearrange("b h j -> b (h j)"), in_=rows[:])

@@ -27,7 +27,7 @@ STEPS = LAYERS * BLOCKS * GATES
 MATRIX_WORDS = PARITIES * PASSES * P
 STEP_WORDS = MATRICES * MATRIX_WORDS
 
-LOAD_AHEAD = 4
+LOAD_AHEAD = 8
 
 FLOPS = 2 * P * (GATES * H) * (MATRICES * H) * LAYERS
 
@@ -45,8 +45,8 @@ def tile_multilayerlstmcell_pb_kernel(
         operand_pool = stack.enter_context(tc.tile_pool(name="operand", bufs=4))
         gate_pool = stack.enter_context(tc.tile_pool(name="gate", bufs=2))
         store_pool = stack.enter_context(tc.tile_pool(name="store", bufs=2 * BLOCKS))
-        bank_pool = stack.enter_context(tc.psum_pool(name="banks", bufs=5))
-        sum_pool = stack.enter_context(tc.psum_pool(name="sums", bufs=3))
+        bank_pool = stack.enter_context(tc.psum_pool(name="banks", bufs=6))
+        sum_pool = stack.enter_context(tc.psum_pool(name="sums", bufs=2))
         stack.enter_context(tc.manual_schedule())
 
         identity = keep.tile([P, P], F32, name="identity")
@@ -96,11 +96,13 @@ def tile_multilayerlstmcell_pb_kernel(
                 rows = weights[j, first : first + BLOCK, :].rearrange(
                     "(r e) k -> r (e k)", e=PARITIES
                 )
-                pieces = PARITIES if s == 0 and not raw_of[s] else 1
-                width = PARITIES * H // pieces
-                for n in range(pieces):
-                    columns = slice(n * width, (n + 1) * width)
-                    nc.sync.dma_start(out=raw[:, columns], in_=rows[:, columns])
+                ends = [0, PARITIES * H]
+                if s == 0 and not raw_of[s]:
+                    ends = [0, H, 2 * H]
+                if s == STEPS - 1 and raw_of[s]:
+                    ends = [0, H, H + H // 2, 2 * H]
+                for a, b in zip(ends, ends[1:]):
+                    nc.sync.dma_start(out=raw[:, a:b], in_=rows[:, a:b])
                 raw_of[s].append(raw)
 
         load(0)
@@ -129,7 +131,7 @@ def tile_multilayerlstmcell_pb_kernel(
             h0_by_pass = h0_grouped[:].rearrange(
                 "p (j g b t) -> p g j b t", j=LAYERS, g=PASSES, t=4
             )
-            for g, copy in enumerate((nc.vector.tensor_copy, nc.scalar.copy)):
+            for g, copy in enumerate((nc.scalar.copy, nc.scalar.copy)):
                 bank = transpose_into_bank(state_blocks(h0_sb[:].bitcast(F32), g))
                 copy(
                     out=h0_by_pass[:, g],
@@ -178,6 +180,19 @@ def tile_multilayerlstmcell_pb_kernel(
         def place(s):
             return s // (BLOCKS * GATES), (s // GATES) % BLOCKS, s % GATES
 
+        def transpose_piece(s, m, e, passes, copy):
+            words = raw_of[s][m][:].bitcast(F32)
+            blocks = row_blocks(words[:, e * ROW_WORDS : (e + 1) * ROW_WORDS])
+            bank = transpose_into_bank(blocks[2 * passes[0] : 2 * passes[-1] + 2])
+            first = ((m * PARITIES + e) * PASSES + passes[0]) * 2 * P
+            width = 2 * P * len(passes)
+            copy(
+                out=grouped_of[s][:].bitcast(F32)[:, first : first + width].rearrange(
+                    "p (g r u) -> p g r u", g=len(passes), u=2
+                ),
+                in_=bank[:, 0:width].rearrange("p (g u r) -> p g r u", g=len(passes), u=2),
+            )
+
         def transpose(s, m, shared=False):
             if s not in grouped_of:
                 grouped_of[s] = grouped_pool.tile(
@@ -190,17 +205,17 @@ def tile_multilayerlstmcell_pb_kernel(
                 bank = transpose_into_bank(
                     row_blocks(words[:, e * ROW_WORDS : (e + 1) * ROW_WORDS])
                 )
-                on_vector = n % 2 == 1 if shared else n == MATRICES * PARITIES - 1
+                on_vector = n % 2 == 1 if shared else n == 2
                 copy = nc.vector.tensor_copy if on_vector else nc.scalar.copy
                 regroup(copy, grouped_words[:, n * BANK : (n + 1) * BANK], bank)
 
-        def quantise(s, m):
+        def quantise(s, m, first=0, last=MATRIX_WORDS):
             if s not in operand_of:
                 codes = operand_pool.tile([P, STEP_WORDS], U32, name="codes", align_bytes=64)
                 scales = operand_pool.tile([P, STEP_WORDS], U8, name="scales", align_bytes=64)
                 operand_of[s] = (codes, scales)
             codes, scales = operand_of[s]
-            first, last = m * MATRIX_WORDS, (m + 1) * MATRIX_WORDS
+            first, last = m * MATRIX_WORDS + first, m * MATRIX_WORDS + last
             nc.vector.quantize_mx(
                 out=codes[:, first:last].bitcast(FP8X4),
                 scales=scales[:, first:last],
@@ -210,7 +225,7 @@ def tile_multilayerlstmcell_pb_kernel(
         def multiply(s):
             j, v, q = place(s)
             codes, scales = operand_of[s]
-            sums = sum_pool.tile([P, PARITIES * P], F32, name="sums")
+            sums = sum_pool.tile([P, BANK], F32, name="sums")
             sums_of[s] = sums
             for e in range(PARITIES):
                 column = e * P
@@ -227,17 +242,35 @@ def tile_multilayerlstmcell_pb_kernel(
                             stop=(m == MATRICES - 1 and g == PASSES - 1),
                         )
 
-        def activate(s):
+        def multiply_part(s, e, m, passes=range(PASSES)):
+            j, v, q = place(s)
+            codes, scales = operand_of[s]
+            if (s, e) not in sums_of:
+                sums_of[(s, e)] = sum_pool.tile([P, BANK], F32, name="sums")
+            moving_codes, moving_scales = (states[j], inputs[j])[m]
+            for g in passes:
+                first = ((m * PARITIES + e) * PASSES + g) * P
+                nc.tensor.matmul_mx(
+                    out=sums_of[(s, e)][:, 0:P],
+                    lhsT=codes[:, first : first + P].bitcast(FP8X4),
+                    lhsT_scale=scales[:, first : first + P],
+                    rhs=moving_codes[:, g * P : (g + 1) * P].bitcast(FP8X4),
+                    rhs_scale=moving_scales[:, g * P : (g + 1) * P],
+                    start=(m == 0 and g == 0),
+                    stop=(m == MATRICES - 1 and g == PASSES - 1),
+                )
+
+        def activate(s, e=None):
             j, v, q = place(s)
             if q == 0:
                 gates_of[(j, v)] = gate_pool.tile([P, GATES * BLOCK], F32, name="gates")
             gates = gates_of[(j, v)]
-            for e in range(PARITIES):
-                column = e * P
+            for e in range(PARITIES) if e is None else [e]:
+                sums = sums_of[(s, e)][:, 0:P] if (s, e) in sums_of else sums_of[s][:, e * P : (e + 1) * P]
                 step_bias = ((j * GATES + q) * BLOCKS + v) * PARITIES + e
                 nc.scalar.activation(
                     out=gates[:, q * BLOCK + e * P : q * BLOCK + (e + 1) * P],
-                    in_=sums_of[s][:, column : column + P],
+                    in_=sums,
                     func=ACT.Tanh if q == 2 else ACT.Sigmoid,
                     bias=bias[:, step_bias : step_bias + 1],
                 )
@@ -278,17 +311,17 @@ def tile_multilayerlstmcell_pb_kernel(
             nc.scalar.activation(out=tanh_cell[:], in_=block_of(cell_t, j, v), func=ACT.Tanh)
             gates_of[(j, v, "tanh_cell")] = tanh_cell
 
-        def make_hidden(j, v):
+        def make_hidden(j, v, first=0, last=BLOCK):
             nc.vector.tensor_tensor(
-                out=block_of(hidden_t, j, v),
-                in0=gate(j, v, 3),
-                in1=gates_of[(j, v, "tanh_cell")][:],
+                out=block_of(hidden_t, j, v)[:, first:last],
+                in0=gate(j, v, 3)[:, first:last],
+                in1=gates_of[(j, v, "tanh_cell")][:, first:last],
                 op=ALU.mult,
             )
 
         def group_hidden(g):
             columns = slice(g * 4 * P, (g + 1) * 4 * P)
-            nc.vector.tensor_copy(
+            nc.scalar.copy(
                 out=hidden_grouped[:, columns].rearrange("p (b t) -> p b t", t=4),
                 in_=hidden_t[0][:, columns].rearrange("p (t b) -> p b t", t=4),
             )
@@ -302,26 +335,31 @@ def tile_multilayerlstmcell_pb_kernel(
 
         finished = []
 
-        def transpose_back(v, planes, out, copy):
+        def transpose_back(v, planes, out, copy, pieces=1):
             bank = transpose_into_bank(
                 [
                     planes[layer][:, (v * PARITIES + e) * P : (v * PARITIES + e + 1) * P]
-                    for e in range(PARITIES)
                     for layer in range(LAYERS)
+                    for e in range(PARITIES)
                 ]
             )
             rows = store_pool.tile([P, BLOCK * LAYERS], F32, name="rows")
-            copy(
-                out=rows[:].rearrange("b (r t) -> b r t", t=4),
-                in_=bank[:].rearrange("b (t r) -> b r t", t=4),
-            )
-            finished.append((out[:, v * BLOCK : (v + 1) * BLOCK, :], rows))
+            by_row = bank[:].rearrange("b (j e r) -> b r e j", j=LAYERS, e=PARITIES)
+            for n in range(pieces):
+                r = slice(n * P // pieces, (n + 1) * P // pieces)
+                columns = slice(n * 4 * P // pieces, (n + 1) * 4 * P // pieces)
+                copy(
+                    out=rows[:, columns].rearrange("b (r e j) -> b r e j", e=PARITIES, j=LAYERS),
+                    in_=by_row[:, r],
+                )
+                h = v * BLOCK + n * BLOCK // pieces
+                finished.append((out[:, h : h + BLOCK // pieces, :], rows[:, columns]))
 
         def cell_back(v, copy=nc.vector.tensor_copy):
             transpose_back(v, cell_t, out_1, copy)
 
-        def hidden_back(v):
-            transpose_back(v, hidden_t, out_0, nc.scalar.copy)
+        def hidden_back(v, pieces=1):
+            transpose_back(v, hidden_t, out_0, nc.scalar.copy, pieces)
 
         UPPER = BLOCKS * GATES
         LAST = STEPS - 1
@@ -373,28 +411,37 @@ def tile_multilayerlstmcell_pb_kernel(
                     squash(j, v)
                 if q == 3 and j == 1 and v < BLOCKS - 2:
                     hidden_back(v)
-                    cell_back(v)
+                    cell_back(v, nc.scalar.copy)
         top = (LAYERS - 1, BLOCKS - 1)
+        on_vector, on_scalar = nc.vector.tensor_copy, nc.scalar.copy
         for m in range(MATRICES):
             quantise(LAST - 1, m)
         transpose(LAST, 0, shared=True)
         multiply(LAST - 2)
         activate(LAST - 2)
-        transpose(LAST, 1, shared=True)
-        multiply(LAST - 1)
-        activate(LAST - 1)
-        hidden_back(BLOCKS - 2)
-        cell_back(BLOCKS - 2, nc.scalar.copy)
+        transpose_piece(LAST, 1, 0, range(PASSES), on_scalar)
         keep_cell(*top)
         quantise(LAST, 0)
+        multiply(LAST - 1)
+        transpose_piece(LAST, 1, 1, [0], on_vector)
+        activate(LAST - 1)
+        transpose_piece(LAST, 1, 1, [1], on_scalar)
+        hidden_back(BLOCKS - 2)
+        cell_back(BLOCKS - 2, on_scalar)
+        for e in range(PARITIES):
+            multiply_part(LAST, e, 0)
         make_fresh(*top)
-        quantise(LAST, 1)
+        quantise(LAST, 1, 0, MATRIX_WORDS // 2)
         add_cell(*top)
-        multiply(LAST)
+        quantise(LAST, 1, MATRIX_WORDS // 2, MATRIX_WORDS * 3 // 4)
+        quantise(LAST, 1, MATRIX_WORDS * 3 // 4, MATRIX_WORDS)
+        for e in range(PARITIES):
+            multiply_part(LAST, e, 1)
         squash(*top)
-        activate(LAST)
-        make_hidden(*top)
+        for e in range(PARITIES):
+            activate(LAST, e)
+            make_hidden(*top, e * P, (e + 1) * P)
         cell_back(BLOCKS - 1)
-        hidden_back(BLOCKS - 1)
+        hidden_back(BLOCKS - 1, pieces=2)
         for out_rows, rows in finished:
-            nc.sync.dma_start(out=out_rows.rearrange("b h j -> b (h j)"), in_=rows[:])
+            nc.sync.dma_start(out=out_rows.rearrange("b h j -> b (h j)"), in_=rows)

@@ -410,8 +410,8 @@ def tile_multilayerlstmcell_pb_kernel(
                 if q == 2:
                     squash(j, v)
                 if q == 3 and j == 1 and v < BLOCKS - 2:
+                    cell_back(v)
                     hidden_back(v)
-                    cell_back(v, nc.scalar.copy)
         top = (LAYERS - 1, BLOCKS - 1)
         on_vector, on_scalar = nc.vector.tensor_copy, nc.scalar.copy
         for m in range(MATRICES):

@@ -116,8 +116,9 @@ def tile_multilayerlstmcell_pb_kernel(
             out=bias_rows[STEPS : 2 * STEPS, :],
             in_=b_hh.rearrange("j (s c) -> (j s) c", c=BLOCK),
         )
+        load(2)
         nc.sync.dma_start(out=c0_sb[:], in_=c0.rearrange("b h j -> b (h j)"))
-        for s in range(2, LOAD_AHEAD):
+        for s in range(3, LOAD_AHEAD):
             load(s)
 
         inputs = [moving_operand("input%d" % j) for j in range(LAYERS)]
@@ -152,7 +153,7 @@ def tile_multilayerlstmcell_pb_kernel(
         c0_t = keep.tile([P, H * LAYERS], BF16, name="c0_t")
         c0_by_layer = c0_t[:].rearrange("p (n j) -> p j n", j=LAYERS)
 
-        def transpose_bias_and_cell():
+        def transpose_bias():
             pairs_bank = bank_pool.tile([P, BANK], F32, name="bank")
             nc.tensor.transpose(pairs_bank[:, 0:P], bias_rows[:].bitcast(F32), identity[:])
             nc.vector.tensor_copy(out=bias_pairs[:].bitcast(F32), in_=pairs_bank[:, 0:P])
@@ -162,6 +163,8 @@ def tile_multilayerlstmcell_pb_kernel(
                 in1=bias_pairs[:, PARITIES * STEPS : 2 * PARITIES * STEPS],
                 op=ALU.add,
             )
+
+        def transpose_cell():
             for g in range(PASSES):
                 cell_bank = transpose_into_bank(state_blocks(c0_sb[:].bitcast(F32), g))
                 nc.scalar.copy(
@@ -393,7 +396,9 @@ def tile_multilayerlstmcell_pb_kernel(
             if s == 0:
                 make_moving_operands()
             if s == 1:
-                transpose_bias_and_cell()
+                transpose_bias()
+            if s == 2:
+                transpose_cell()
             if s + LOAD_AHEAD < STEPS:
                 load(s + LOAD_AHEAD)
             if s >= 3:

from contextlib import ExitStack

import concourse.mybir as mybir
from concourse.masks import make_identity

F32 = mybir.dt.float32
BF16 = mybir.dt.bfloat16
U32 = mybir.dt.uint32
U8 = mybir.dt.uint8
FP8X4 = mybir.dt.float8_e4m3fn_x4
ACT = mybir.ActivationFunctionType
ALU = mybir.AluOpType

P = 128
H = 1024
LAYERS = 2
GATES = 4
PASSES = H // (4 * P)
PARITIES = 2
BLOCK = PARITIES * P
BLOCKS = H // BLOCK
ROW_WORDS = H // 2
BANK = 512
MATRICES = 2

STEPS = LAYERS * BLOCKS * GATES
MATRIX_WORDS = PARITIES * PASSES * P
STEP_WORDS = MATRICES * MATRIX_WORDS

LOAD_AHEAD = 8

FLOPS = 2 * P * (GATES * H) * (MATRICES * H) * LAYERS


def tile_multilayerlstmcell_pb_kernel(
    tc, lstm_input, h0, c0, W_ih, W_hh, b_ih, b_hh, out_0, out_1
):
    nc = tc.nc
    with ExitStack() as stack:
        keep = stack.enter_context(tc.tile_pool(name="keep", bufs=1))
        raw_pool = stack.enter_context(
            tc.tile_pool(name="raw", bufs=MATRICES * (LOAD_AHEAD + 1))
        )
        grouped_pool = stack.enter_context(tc.tile_pool(name="grouped", bufs=3))
        operand_pool = stack.enter_context(tc.tile_pool(name="operand", bufs=4))
        gate_pool = stack.enter_context(tc.tile_pool(name="gate", bufs=2))
        store_pool = stack.enter_context(tc.tile_pool(name="store", bufs=2 * BLOCKS))
        bank_pool = stack.enter_context(tc.psum_pool(name="banks", bufs=6))
        sum_pool = stack.enter_context(tc.psum_pool(name="sums", bufs=2))
        stack.enter_context(tc.manual_schedule())

        identity = keep.tile([P, P], F32, name="identity")
        make_identity(nc, identity[:])
        table_warmer = keep.tile([P, 1], F32, name="table_warmer")
        nc.scalar.activation(out=table_warmer[:], in_=identity[:, 0:1], func=ACT.Sigmoid)

        def transpose_into_bank(word_blocks):
            bank = bank_pool.tile([P, BANK], F32, name="bank")
            for i, block in enumerate(word_blocks):
                nc.tensor.transpose(bank[:, i * P : (i + 1) * P], block, identity[:])
            return bank

        def row_blocks(words):
            return [words[:, w * P : (w + 1) * P] for w in range(ROW_WORDS // P)]

        def regroup(copy, grouped_words, bank):
            copy(
                out=grouped_words.rearrange("p (g r u) -> p g r u", g=PASSES, u=2),
                in_=bank[:].rearrange("p (g u r) -> p g r u", g=PASSES, u=2),
            )

        def state_blocks(state_words, g):
            by_parity = state_words.rearrange(
                "b (w p e) -> b w e p", w=BLOCKS, e=PARITIES
            )
            return [by_parity[:, 2 * g + t // 2, t % 2, :] for t in range(4)]

        def moving_operand(name):
            codes = keep.tile([P, PASSES * P], U32, name=name + "_codes", align_bytes=64)
            scales = keep.tile([P, PASSES * P], U8, name=name + "_scales", align_bytes=64)
            return codes, scales

        x_sb = keep.tile([P, H], BF16, name="x_sb")
        h0_sb = keep.tile([P, H * LAYERS], BF16, name="h0_sb")
        c0_sb = keep.tile([P, H * LAYERS], BF16, name="c0_sb")
        bias_rows = keep.tile([P, BLOCK], BF16, name="bias_rows")
        nc.vector.memset(bias_rows[2 * STEPS : P, :], 0.0)
        raw_of = {}

        def load(s):
            j, v, q = s // (BLOCKS * GATES), (s // GATES) % BLOCKS, s % GATES
            first = q * H + v * BLOCK
            raw_of[s] = []
            for weights in (W_hh, W_ih):
                raw = raw_pool.tile([P, PARITIES * H], BF16, name="raw")
                rows = weights[j, first : first + BLOCK, :].rearrange(
                    "(r e) k -> r (e k)", e=PARITIES
                )
                ends = [0, PARITIES * H]
                if s == 0 and not raw_of[s]:
                    ends = [0, H, 2 * H]
                if s == STEPS - 1 and raw_of[s]:
                    ends = [0, H, H + H // 2, 2 * H]
                for a, b in zip(ends, ends[1:]):
                    nc.sync.dma_start(out=raw[:, a:b], in_=rows[:, a:b])
                raw_of[s].append(raw)

        load(0)
        nc.sync.dma_start(out=x_sb[:], in_=lstm_input)
        nc.sync.dma_start(out=h0_sb[:], in_=h0.rearrange("b h j -> b (h j)"))
        load(1)
        nc.sync.dma_start(
            out=bias_rows[0:STEPS, :], in_=b_ih.rearrange("j (s c) -> (j s) c", c=BLOCK)
        )
        nc.sync.dma_start(
            out=bias_rows[STEPS : 2 * STEPS, :],
            in_=b_hh.rearrange("j (s c) -> (j s) c", c=BLOCK),
        )
        load(2)
        nc.sync.dma_start(out=c0_sb[:], in_=c0.rearrange("b h j -> b (h j)"))
        for s in range(3, LOAD_AHEAD):
            load(s)

        inputs = [moving_operand("input%d" % j) for j in range(LAYERS)]
        states = [moving_operand("state%d" % j) for j in range(LAYERS)]
        x_grouped = keep.tile([P, H], BF16, name="x_grouped", align_bytes=64)
        h0_grouped = keep.tile([P, LAYERS * H], BF16, name="h0_grouped", align_bytes=64)

        def make_moving_operands():
            bank = transpose_into_bank(row_blocks(x_sb[:].bitcast(F32)))
            regroup(nc.vector.tensor_copy, x_grouped[:].bitcast(F32), bank)
            h0_by_pass = h0_grouped[:].rearrange(
                "p (j g b t) -> p g j b t", j=LAYERS, g=PASSES, t=4
            )
            for g, copy in enumerate((nc.scalar.copy, nc.scalar.copy)):
                bank = transpose_into_bank(state_blocks(h0_sb[:].bitcast(F32), g))
                copy(
                    out=h0_by_pass[:, g],
                    in_=bank[:].bitcast(BF16).rearrange("p (t b j) -> p j b t", t=4, j=LAYERS),
                )
            nc.vector.quantize_mx(
                out=inputs[0][0][:].bitcast(FP8X4), scales=inputs[0][1][:], in_=x_grouped[:]
            )
            for j in range(LAYERS):
                nc.vector.quantize_mx(
                    out=states[j][0][:].bitcast(FP8X4),
                    scales=states[j][1][:],
                    in_=h0_grouped[:, j * H : (j + 1) * H],
                )

        bias_pairs = keep.tile([P, PARITIES * P], BF16, name="bias_pairs")
        bias = keep.tile([P, PARITIES * STEPS], F32, name="bias")
        c0_t = keep.tile([P, H * LAYERS], BF16, name="c0_t")
        c0_by_layer = c0_t[:].rearrange("p (n j) -> p j n", j=LAYERS)

        def transpose_bias():
            pairs_bank = bank_pool.tile([P, BANK], F32, name="bank")
            nc.tensor.transpose(pairs_bank[:, 0:P], bias_rows[:].bitcast(F32), identity[:])
            nc.vector.tensor_copy(out=bias_pairs[:].bitcast(F32), in_=pairs_bank[:, 0:P])
            nc.vector.tensor_tensor(
                out=bias[:],
                in0=bias_pairs[:, 0 : PARITIES * STEPS],
                in1=bias_pairs[:, PARITIES * STEPS : 2 * PARITIES * STEPS],
                op=ALU.add,
            )

        def transpose_cell():
            for g in range(PASSES):
                cell_bank = transpose_into_bank(state_blocks(c0_sb[:].bitcast(F32), g))
                nc.scalar.copy(
                    out=c0_t[:].bitcast(F32)[:, g * BANK : (g + 1) * BANK], in_=cell_bank[:]
                )

        hidden_t = [keep.tile([P, H], F32, name="hidden_t%d" % j) for j in range(LAYERS)]
        cell_t = [keep.tile([P, H], F32, name="cell_t%d" % j) for j in range(LAYERS)]
        hidden_grouped = keep.tile([P, H], BF16, name="hidden_grouped", align_bytes=64)

        grouped_of = {}
        operand_of = {}
        gates_of = {}
        sums_of = {}

        def place(s):
            return s // (BLOCKS * GATES), (s // GATES) % BLOCKS, s % GATES

        def transpose_piece(s, m, e, passes, copy):
            words = raw_of[s][m][:].bitcast(F32)
            blocks = row_blocks(words[:, e * ROW_WORDS : (e + 1) * ROW_WORDS])
            bank = transpose_into_bank(blocks[2 * passes[0] : 2 * passes[-1] + 2])
            first = ((m * PARITIES + e) * PASSES + passes[0]) * 2 * P
            width = 2 * P * len(passes)
            copy(
                out=grouped_of[s][:].bitcast(F32)[:, first : first + width].rearrange(
                    "p (g r u) -> p g r u", g=len(passes), u=2
                ),
                in_=bank[:, 0:width].rearrange("p (g u r) -> p g r u", g=len(passes), u=2),
            )

        def transpose(s, m, shared=False):
            if s not in grouped_of:
                grouped_of[s] = grouped_pool.tile(
                    [P, 4 * STEP_WORDS], BF16, name="grouped", align_bytes=64
                )
            grouped_words = grouped_of[s][:].bitcast(F32)
            words = raw_of[s][m][:].bitcast(F32)
            for e in range(PARITIES):
                n = m * PARITIES + e
                bank = transpose_into_bank(
                    row_blocks(words[:, e * ROW_WORDS : (e + 1) * ROW_WORDS])
                )
                on_vector = n % 2 == 1 if shared else n == 2
                copy = nc.vector.tensor_copy if on_vector else nc.scalar.copy
                regroup(copy, grouped_words[:, n * BANK : (n + 1) * BANK], bank)

        def quantise(s, m, first=0, last=MATRIX_WORDS):
            if s not in operand_of:
                codes = operand_pool.tile([P, STEP_WORDS], U32, name="codes", align_bytes=64)
                scales = operand_pool.tile([P, STEP_WORDS], U8, name="scales", align_bytes=64)
                operand_of[s] = (codes, scales)
            codes, scales = operand_of[s]
            first, last = m * MATRIX_WORDS + first, m * MATRIX_WORDS + last
            nc.vector.quantize_mx(
                out=codes[:, first:last].bitcast(FP8X4),
                scales=scales[:, first:last],
                in_=grouped_of[s][:, 4 * first : 4 * last],
            )

        def multiply(s):
            j, v, q = place(s)
            codes, scales = operand_of[s]
            sums = sum_pool.tile([P, BANK], F32, name="sums")
            sums_of[s] = sums
            for e in range(PARITIES):
                column = e * P
                for m, (moving_codes, moving_scales) in enumerate((states[j], inputs[j])):
                    for g in range(PASSES):
                        first = ((m * PARITIES + e) * PASSES + g) * P
                        nc.tensor.matmul_mx(
                            out=sums[:, column : column + P],
                            lhsT=codes[:, first : first + P].bitcast(FP8X4),
                            lhsT_scale=scales[:, first : first + P],
                            rhs=moving_codes[:, g * P : (g + 1) * P].bitcast(FP8X4),
                            rhs_scale=moving_scales[:, g * P : (g + 1) * P],
                            start=(m == 0 and g == 0),
                            stop=(m == MATRICES - 1 and g == PASSES - 1),
                        )

        def multiply_part(s, e, m, passes=range(PASSES)):
            j, v, q = place(s)
            codes, scales = operand_of[s]
            if (s, e) not in sums_of:
                sums_of[(s, e)] = sum_pool.tile([P, BANK], F32, name="sums")
            moving_codes, moving_scales = (states[j], inputs[j])[m]
            for g in passes:
                first = ((m * PARITIES + e) * PASSES + g) * P
                nc.tensor.matmul_mx(
                    out=sums_of[(s, e)][:, 0:P],
                    lhsT=codes[:, first : first + P].bitcast(FP8X4),
                    lhsT_scale=scales[:, first : first + P],
                    rhs=moving_codes[:, g * P : (g + 1) * P].bitcast(FP8X4),
                    rhs_scale=moving_scales[:, g * P : (g + 1) * P],
                    start=(m == 0 and g == 0),
                    stop=(m == MATRICES - 1 and g == PASSES - 1),
                )

        def activate(s, e=None):
            j, v, q = place(s)
            if q == 0:
                gates_of[(j, v)] = gate_pool.tile([P, GATES * BLOCK], F32, name="gates")
            gates = gates_of[(j, v)]
            for e in range(PARITIES) if e is None else [e]:
                sums = sums_of[(s, e)][:, 0:P] if (s, e) in sums_of else sums_of[s][:, e * P : (e + 1) * P]
                step_bias = ((j * GATES + q) * BLOCKS + v) * PARITIES + e
                nc.scalar.activation(
                    out=gates[:, q * BLOCK + e * P : q * BLOCK + (e + 1) * P],
                    in_=sums,
                    func=ACT.Tanh if q == 2 else ACT.Sigmoid,
                    bias=bias[:, step_bias : step_bias + 1],
                )

        def gate(j, v, q):
            return gates_of[(j, v)][:, q * BLOCK : (q + 1) * BLOCK]

        def block_of(planes, j, v):
            return planes[j][:, v * BLOCK : (v + 1) * BLOCK]

        def keep_cell(j, v):
            kept = gate_pool.tile([P, BLOCK], F32, name="kept")
            nc.vector.tensor_tensor(
                out=kept[:],
                in0=gate(j, v, 1),
                in1=c0_by_layer[:, j, v * BLOCK : (v + 1) * BLOCK],
                op=ALU.mult,
            )
            gates_of[(j, v, "kept")] = kept

        def make_fresh(j, v):
            fresh = gate_pool.tile([P, BLOCK], F32, name="fresh")
            nc.vector.tensor_tensor(
                out=fresh[:], in0=gate(j, v, 0), in1=gate(j, v, 2), op=ALU.mult
            )
            gates_of[(j, v, "fresh")] = fresh

        def add_cell(j, v):
            nc.vector.tensor_tensor(
                out=block_of(cell_t, j, v),
                in0=gates_of[(j, v, "kept")][:],
                in1=gates_of[(j, v, "fresh")][:],
                op=ALU.add,
            )

        def squash(j, v):
            tanh_cell = gate_pool.tile([P, BLOCK], F32, name="tanh_cell")
            nc.scalar.activation(out=tanh_cell[:], in_=block_of(cell_t, j, v), func=ACT.Tanh)
            gates_of[(j, v, "tanh_cell")] = tanh_cell

        def make_hidden(j, v, first=0, last=BLOCK):
            nc.vector.tensor_tensor(
                out=block_of(hidden_t, j, v)[:, first:last],
                in0=gate(j, v, 3)[:, first:last],
                in1=gates_of[(j, v, "tanh_cell")][:, first:last],
                op=ALU.mult,
            )

        def group_hidden(g):
            columns = slice(g * 4 * P, (g + 1) * 4 * P)
            nc.scalar.copy(
                out=hidden_grouped[:, columns].rearrange("p (b t) -> p b t", t=4),
                in_=hidden_t[0][:, columns].rearrange("p (t b) -> p b t", t=4),
            )

        def quantise_hidden(g):
            nc.vector.quantize_mx(
                out=inputs[1][0][:, g * P : (g + 1) * P].bitcast(FP8X4),
                scales=inputs[1][1][:, g * P : (g + 1) * P],
                in_=hidden_grouped[:, g * 4 * P : (g + 1) * 4 * P],
            )

        finished = []

        def transpose_back(v, planes, out, copy, pieces=1):
            bank = transpose_into_bank(
                [
                    planes[layer][:, (v * PARITIES + e) * P : (v * PARITIES + e + 1) * P]
                    for layer in range(LAYERS)
                    for e in range(PARITIES)
                ]
            )
            rows = store_pool.tile([P, BLOCK * LAYERS], F32, name="rows")
            by_row = bank[:].rearrange("b (j e r) -> b r e j", j=LAYERS, e=PARITIES)
            for n in range(pieces):
                r = slice(n * P // pieces, (n + 1) * P // pieces)
                columns = slice(n * 4 * P // pieces, (n + 1) * 4 * P // pieces)
                copy(
                    out=rows[:, columns].rearrange("b (r e j) -> b r e j", e=PARITIES, j=LAYERS),
                    in_=by_row[:, r],
                )
                h = v * BLOCK + n * BLOCK // pieces
                finished.append((out[:, h : h + BLOCK // pieces, :], rows[:, columns]))

        def cell_back(v, copy=nc.vector.tensor_copy):
            transpose_back(v, cell_t, out_1, copy)

        def hidden_back(v, pieces=1):
            transpose_back(v, hidden_t, out_0, nc.scalar.copy, pieces)

        UPPER = BLOCKS * GATES
        LAST = STEPS - 1

        def update_first(s):
            j, v, q = place(s)
            if s == UPPER or (j == 0 and q == 0 and v == 2):
                quantise_hidden(0 if s < UPPER else 1)
            if q == 1:
                keep_cell(j, v)
            if q == 2:
                make_fresh(j, v)
            if q == 3:
                make_hidden(j, v)

        def update_last(s):
            j, v, q = place(s)
            if q == 2:
                add_cell(j, v)
            if q == 3 and j == 0 and v % 2 == 1:
                group_hidden(v // 2)

        for s in range(LAST):
            if s >= 1:
                for m in range(MATRICES):
                    quantise(s - 1, m)
            if s >= 3:
                update_first(s - 3)
            for m in range(MATRICES):
                transpose(s, m, shared=s == 0)
            if s == 0:
                make_moving_operands()
            if s == 1:
                transpose_bias()
            if s == 2:
                transpose_cell()
            if s + LOAD_AHEAD < STEPS:
                load(s + LOAD_AHEAD)
            if s >= 3:
                update_last(s - 3)
            ripe = [] if s - 2 == UPPER else [s - 2] if s - 2 != UPPER + 1 else [s - 3, s - 2]
            for r in ripe:
                if r >= 0:
                    multiply(r)
            for r in ripe:
                if r >= 0:
                    activate(r)
            if s >= 3:
                j, v, q = place(s - 3)
                if q == 2:
                    squash(j, v)
                if q == 3 and j == 1 and v < BLOCKS - 2:
                    cell_back(v)
                    hidden_back(v)
        top = (LAYERS - 1, BLOCKS - 1)
        on_vector, on_scalar = nc.vector.tensor_copy, nc.scalar.copy
        for m in range(MATRICES):
            quantise(LAST - 1, m)
        transpose(LAST, 0, shared=True)
        multiply(LAST - 2)
        activate(LAST - 2)
        transpose_piece(LAST, 1, 0, range(PASSES), on_scalar)
        keep_cell(*top)
        quantise(LAST, 0)
        multiply(LAST - 1)
        transpose_piece(LAST, 1, 1, [0], on_vector)
        activate(LAST - 1)
        transpose_piece(LAST, 1, 1, [1], on_scalar)
        hidden_back(BLOCKS - 2)
        cell_back(BLOCKS - 2, on_scalar)
        for e in range(PARITIES):
            multiply_part(LAST, e, 0)
        make_fresh(*top)
        quantise(LAST, 1, 0, MATRIX_WORDS // 2)
        add_cell(*top)
        quantise(LAST, 1, MATRIX_WORDS // 2, MATRIX_WORDS * 3 // 4)
        quantise(LAST, 1, MATRIX_WORDS * 3 // 4, MATRIX_WORDS)
        for e in range(PARITIES):
            multiply_part(LAST, e, 1)
        squash(*top)
        for e in range(PARITIES):
            activate(LAST, e)
            make_hidden(*top, e * P, (e + 1) * P)
        cell_back(BLOCKS - 1)
        hidden_back(BLOCKS - 1, pieces=2)
        for out_rows, rows in finished:
            nc.sync.dma_start(out=out_rows.rearrange("b h j -> b (h j)"), in_=rows)
